import numpy as np
import ml_dtypes

BF16 = ml_dtypes.bfloat16


def bf(x):
    return np.asarray(x, np.float32).astype(BF16)


def f32(x):
    return np.asarray(x, np.float32)


def f64(x):
    return np.asarray(x).astype(np.float64)


def striped(idx):
    return np.tile(idx.reshape(-1, 16).T, (8, 1))


V, D, B, T, N, H, K = 256, 512, 4, 512, 2048, 128, 16
FREQ = 60.0


def sigmoid(v):
    return 1.0 / (1.0 + np.exp(-v))


def setup_inputs():
    ph = FREQ * 2.0 * np.pi * np.linspace(0.0, 1.0, T)
    return {
        "emb": f32(3.0 * np.random.standard_normal((D, V))),
        "coh": f32(np.cos(ph[:, None] - ph[None, :])),
        "w1": f32(0.25 * np.random.standard_normal((D, D))),
        "fw1": f32(0.25 * np.random.standard_normal((D, D))),
        "b1": f32(0.2 * np.random.standard_normal((D, 1))),
        "w2": f32(np.random.standard_normal((D, D)) / np.sqrt(D)),
        "fw2": f32(np.random.standard_normal((D, D)) / np.sqrt(D)),
        "b2": f32(0.2 * np.random.standard_normal((D, 1))),
        "offs": striped(np.concatenate([np.random.permutation(V)[:H] for _ in range(K)])),
    }


def reference(emb, coh, w1, fw1, b1, w2, fw2, b2, offs):
    idx = offs[:16].T.reshape(-1)
    x = f64(emb)[:, idx].reshape(D, B, T)
    mask = sigmoid(f64(coh))
    att = (x @ mask).reshape(D, N) / T
    h = np.tanh((f64(w1) + f64(fw1)).T @ att + f64(b1))
    return np.tanh((f64(w2) + f64(fw2)).T @ h + f64(b2))

@@ -1,0 +1,117 @@
+import concourse.mybir as mybir
+
+F32 = mybir.dt.float32
+BF16 = mybir.dt.bfloat16
+U16 = mybir.dt.uint16
+COPY = mybir.ActivationFunctionType.Copy
+SIGMOID = mybir.ActivationFunctionType.Sigmoid
+TANH = mybir.ActivationFunctionType.Tanh
+ADD = mybir.AluOpType.add
+
+P = 128
+VOCAB = 256
+FEATURES = 512
+TEXTS = 4
+TOKENS = 512
+BLOCKS = FEATURES // P
+PIECE = VOCAB
+FLOPS = 3 * 2 * FEATURES * FEATURES * TEXTS * TOKENS
+
+
+def block(i):
+    return slice(i * P, (i + 1) * P)
+
+
+def tile_neuronsv2textclassifier_b_kernel(tc, emb, coh, w1, fw1, b1, w2, fw2, b2, offs, out):
+    nc = tc.nc
+    with (
+        tc.tile_pool(name="held", bufs=1) as held,
+        tc.psum_pool(name="psum", bufs=8) as psum,
+    ):
+        offsets = held.tile([P, TEXTS * TOKENS // 16], U16, name="offsets")
+        table = [held.tile([P, VOCAB], F32, name=f"table{d}") for d in range(BLOCKS)]
+        slow1 = [held.tile([P, FEATURES], F32, name=f"slow1_{d}") for d in range(BLOCKS)]
+        fast1 = [held.tile([P, FEATURES], F32, name=f"fast1_{d}") for d in range(BLOCKS)]
+        slow2 = [held.tile([P, FEATURES], F32, name=f"slow2_{m}") for m in range(BLOCKS)]
+        fast2 = [held.tile([P, FEATURES], F32, name=f"fast2_{m}") for m in range(BLOCKS)]
+        weights1 = [held.tile([P, FEATURES], BF16, name=f"weights1_{d}") for d in range(BLOCKS)]
+        weights2 = [held.tile([P, FEATURES], BF16, name=f"weights2_{m}") for m in range(BLOCKS)]
+        coherence = [held.tile([P, TOKENS], F32, name=f"coherence{s}") for s in range(BLOCKS)]
+        mask = [held.tile([P, TOKENS], BF16, name=f"mask{s}") for s in range(BLOCKS)]
+        bias1 = held.tile([P, BLOCKS], F32, name="bias1")
+        bias2 = held.tile([P, BLOCKS], F32, name="bias2")
+        picked = [[held.tile([P, TOKENS], F32, name=f"picked{r}_{d}") for d in range(BLOCKS)] for r in range(TEXTS)]
+        x = [[held.tile([P, TOKENS], BF16, name=f"x{r}_{d}") for d in range(BLOCKS)] for r in range(TEXTS)]
+        y = [[held.tile([P, FEATURES], BF16, name=f"y{r}_{s}") for s in range(BLOCKS)] for r in range(TEXTS)]
+        h = [[held.tile([P, TOKENS], BF16, name=f"h{r}_{m}") for m in range(BLOCKS)] for r in range(TEXTS)]
+        result = [[held.tile([P, TOKENS], F32, name=f"result{r}_{e}") for e in range(BLOCKS)] for r in range(TEXTS)]
+
+        nc.sync.dma_start(offsets[:], offs)
+        for d in range(BLOCKS):
+            nc.sync.dma_start(table[d][:], emb[block(d), :])
+            nc.sync.dma_start(slow1[d][:], w1[block(d), :])
+            nc.scalar.dma_start(fast1[d][:], fw1[block(d), :])
+        for s in range(BLOCKS):
+            nc.sync.dma_start(coherence[s][:], coh[block(s), :])
+        with nc.allow_non_contiguous_dma(reason="512 biases, one to a partition, four columns"):
+            nc.gpsimd.dma_start(bias1[:], b1.rearrange("(m p) o -> p (m o)", p=P))
+            nc.gpsimd.dma_start(bias2[:], b2.rearrange("(e p) o -> p (e o)", p=P))
+        for m in range(BLOCKS):
+            nc.gpsimd.dma_start(slow2[m][:], w2[block(m), :])
+            nc.gpsimd.dma_start(fast2[m][:], fw2[block(m), :])
+
+        def look_up(r, d):
+            for first in range(0, TOKENS, PIECE):
+                column = (r * TOKENS + first) // 16
+                nc.scalar.activation(
+                    picked[r][d][:, first : first + PIECE],
+                    table[d][:].indirect(offsets[:, column : column + PIECE // 16]),
+                    COPY,
+                )
+            nc.vector.tensor_copy(x[r][d][:], picked[r][d][:])
+
+        def step_a(r):
+            banks = [psum.tile([P, FEATURES], F32, name="bank") for s in range(BLOCKS)]
+            for d in range(BLOCKS):
+                for s in range(BLOCKS):
+                    nc.tensor.matmul(
+                        banks[s][:], x[r][d][:, block(s)], weights1[d][:], start=(d == 0), stop=(d == BLOCKS - 1)
+                    )
+            for s in range(BLOCKS):
+                nc.vector.tensor_copy(y[r][s][:], banks[s][:])
+
+        def step_b(r):
+            for m in range(BLOCKS):
+                bank = psum.tile([P, TOKENS], F32, name="bank")
+                for s in range(BLOCKS):
+                    nc.tensor.matmul(bank[:], y[r][s][:, block(m)], mask[s][:], start=(s == 0), stop=(s == BLOCKS - 1))
+                nc.scalar.activation(h[r][m][:], bank[:], TANH, bias=bias1[:, m : m + 1], scale=1.0 / TOKENS)
+
+        def step_c(r):
+            for e in range(BLOCKS):
+                bank = psum.tile([P, TOKENS], F32, name="bank")
+                for m in range(BLOCKS):
+                    nc.tensor.matmul(bank[:], weights2[m][:, block(e)], h[r][m][:], start=(m == 0), stop=(m == BLOCKS - 1))
+                nc.scalar.activation(result[r][e][:], bank[:], TANH, bias=bias2[:, e : e + 1])
+                nc.sync.dma_start(out[block(e), r * TOKENS : (r + 1) * TOKENS], result[r][e][:])
+
+        for d in range(BLOCKS):
+            nc.vector.tensor_tensor(weights1[d][:], slow1[d][:], fast1[d][:], ADD)
+            look_up(0, d)
+        step_a(0)
+        for d in range(BLOCKS):
+            look_up(1, d)
+        for s in range(BLOCKS):
+            nc.scalar.activation(mask[s][:], coherence[s][:], SIGMOID)
+        for m in range(BLOCKS):
+            nc.gpsimd.tensor_tensor(weights2[m][:], slow2[m][:], fast2[m][:], ADD)
+        for turn in range(1, TEXTS + 2):
+            if turn < TEXTS:
+                step_a(turn)
+            if turn + 1 < TEXTS:
+                for d in range(BLOCKS):
+                    look_up(turn + 1, d)
+            if turn - 1 < TEXTS:
+                step_b(turn - 1)
+            if turn >= 2:
+                step_c(turn - 2)

@@ -50,15 +50,15 @@ def tile_neuronsv2textclassifier_b_kernel(tc, emb, coh, w1, fw1, b1, w2, fw2, b2
         for d in range(BLOCKS):
             nc.sync.dma_start(table[d][:], emb[block(d), :])
             nc.sync.dma_start(slow1[d][:], w1[block(d), :])
-            nc.scalar.dma_start(fast1[d][:], fw1[block(d), :])
+            nc.sync.dma_start(fast1[d][:], fw1[block(d), :])
         for s in range(BLOCKS):
             nc.sync.dma_start(coherence[s][:], coh[block(s), :])
+        for m in range(BLOCKS):
+            nc.sync.dma_start(slow2[m][:], w2[block(m), :])
+            nc.sync.dma_start(fast2[m][:], fw2[block(m), :])
         with nc.allow_non_contiguous_dma(reason="512 biases, one to a partition, four columns"):
             nc.gpsimd.dma_start(bias1[:], b1.rearrange("(m p) o -> p (m o)", p=P))
             nc.gpsimd.dma_start(bias2[:], b2.rearrange("(e p) o -> p (e o)", p=P))
-        for m in range(BLOCKS):
-            nc.gpsimd.dma_start(slow2[m][:], w2[block(m), :])
-            nc.gpsimd.dma_start(fast2[m][:], fw2[block(m), :])
 
         def look_up(r, d):
             for first in range(0, TOKENS, PIECE):

@@ -46,6 +46,11 @@ def tile_neuronsv2textclassifier_b_kernel(tc, emb, coh, w1, fw1, b1, w2, fw2, b2
         h = [[held.tile([P, TOKENS], BF16, name=f"h{r}_{m}") for m in range(BLOCKS)] for r in range(TEXTS)]
         result = [[held.tile([P, TOKENS], F32, name=f"result{r}_{e}") for e in range(BLOCKS)] for r in range(TEXTS)]
 
+        zeros = held.tile([P, 1], F32, name="zeros")
+        unused = held.tile([P, 1], F32, name="unused")
+        nc.vector.memset(zeros[:], 0.0)
+        nc.scalar.activation(unused[:], zeros[:], SIGMOID)
+
         nc.sync.dma_start(offsets[:], offs)
         for d in range(BLOCKS):
             nc.sync.dma_start(table[d][:], emb[block(d), :])

@@ -73,7 +73,7 @@ def tile_neuronsv2textclassifier_b_kernel(tc, emb, coh, w1, fw1, b1, w2, fw2, b2
                     table[d][:].indirect(offsets[:, column : column + PIECE // 16]),
                     COPY,
                 )
-            nc.vector.tensor_copy(x[r][d][:], picked[r][d][:])
+            nc.gpsimd.tensor_copy(x[r][d][:], picked[r][d][:])
 
         def step_a(r):
             banks = [psum.tile([P, FEATURES], F32, name="bank") for s in range(BLOCKS)]
@@ -108,15 +108,18 @@ def tile_neuronsv2textclassifier_b_kernel(tc, emb, coh, w1, fw1, b1, w2, fw2, b2
             look_up(1, d)
         for s in range(BLOCKS):
             nc.scalar.activation(mask[s][:], coherence[s][:], SIGMOID)
+        step_a(1)
+        for d in range(BLOCKS):
+            look_up(2, d)
         for m in range(BLOCKS):
-            nc.gpsimd.tensor_tensor(weights2[m][:], slow2[m][:], fast2[m][:], ADD)
-        for turn in range(1, TEXTS + 2):
-            if turn < TEXTS:
-                step_a(turn)
-            if turn + 1 < TEXTS:
+            nc.vector.tensor_tensor(weights2[m][:], slow2[m][:], fast2[m][:], ADD)
+        for r in range(TEXTS):
+            step_b(r)
+            if r >= 1:
+                step_c(r - 1)
+            if r + 3 < TEXTS:
                 for d in range(BLOCKS):
-                    look_up(turn + 1, d)
-            if turn - 1 < TEXTS:
-                step_b(turn - 1)
-            if turn >= 2:
-                step_c(turn - 2)
+                    look_up(r + 3, d)
+            if r + 2 < TEXTS:
+                step_a(r + 2)
+        step_c(TEXTS - 1)

@@ -54,6 +54,7 @@ def tile_neuronsv2textclassifier_b_kernel(tc, emb, coh, w1, fw1, b1, w2, fw2, b2
         nc.sync.dma_start(offsets[:], offs)
         for d in range(BLOCKS):
             nc.sync.dma_start(table[d][:], emb[block(d), :])
+        for d in range(BLOCKS):
             nc.sync.dma_start(slow1[d][:], w1[block(d), :])
             nc.sync.dma_start(fast1[d][:], fw1[block(d), :])
         for s in range(BLOCKS):
@@ -86,11 +87,14 @@ def tile_neuronsv2textclassifier_b_kernel(tc, emb, coh, w1, fw1, b1, w2, fw2, b2
                 nc.vector.tensor_copy(y[r][s][:], banks[s][:])
 
         def step_b(r):
+            banks = [psum.tile([P, TOKENS], F32, name="bank") for m in range(BLOCKS)]
+            for s in range(BLOCKS):
+                for m in range(BLOCKS):
+                    nc.tensor.matmul(
+                        banks[m][:], y[r][s][:, block(m)], mask[s][:], start=(s == 0), stop=(s == BLOCKS - 1)
+                    )
             for m in range(BLOCKS):
-                bank = psum.tile([P, TOKENS], F32, name="bank")
-                for s in range(BLOCKS):
-                    nc.tensor.matmul(bank[:], y[r][s][:, block(m)], mask[s][:], start=(s == 0), stop=(s == BLOCKS - 1))
-                nc.scalar.activation(h[r][m][:], bank[:], TANH, bias=bias1[:, m : m + 1], scale=1.0 / TOKENS)
+                nc.scalar.activation(h[r][m][:], banks[m][:], TANH, bias=bias1[:, m : m + 1], scale=1.0 / TOKENS)
 
         def step_c(r):
             for e in range(BLOCKS):
@@ -102,24 +106,16 @@ def tile_neuronsv2textclassifier_b_kernel(tc, emb, coh, w1, fw1, b1, w2, fw2, b2
 
         for d in range(BLOCKS):
             nc.vector.tensor_tensor(weights1[d][:], slow1[d][:], fast1[d][:], ADD)
-            look_up(0, d)
-        step_a(0)
-        for d in range(BLOCKS):
-            look_up(1, d)
+        for r in range(TEXTS):
+            for d in range(BLOCKS):
+                look_up(r, d)
+            step_a(r)
         for s in range(BLOCKS):
             nc.scalar.activation(mask[s][:], coherence[s][:], SIGMOID)
-        step_a(1)
-        for d in range(BLOCKS):
-            look_up(2, d)
         for m in range(BLOCKS):
             nc.vector.tensor_tensor(weights2[m][:], slow2[m][:], fast2[m][:], ADD)
-        for r in range(TEXTS):
+        step_b(0)
+        for r in range(1, TEXTS):
             step_b(r)
-            if r >= 1:
-                step_c(r - 1)
-            if r + 3 < TEXTS:
-                for d in range(BLOCKS):
-                    look_up(r + 3, d)
-            if r + 2 < TEXTS:
-                step_a(r + 2)
+            step_c(r - 1)
         step_c(TEXTS - 1)

@@ -15,6 +15,8 @@ TEXTS = 4
 TOKENS = 512
 BLOCKS = FEATURES // P
 PIECE = VOCAB
+PIECES = TOKENS // PIECE
+PSUM_BANKS = 8
 FLOPS = 3 * 2 * FEATURES * FEATURES * TEXTS * TOKENS
 
 
@@ -26,7 +28,7 @@ def tile_neuronsv2textclassifier_b_kernel(tc, emb, coh, w1, fw1, b1, w2, fw2, b2
     nc = tc.nc
     with (
         tc.tile_pool(name="held", bufs=1) as held,
-        tc.psum_pool(name="psum", bufs=8) as psum,
+        tc.psum_pool(name="psum", bufs=PSUM_BANKS) as psum,
     ):
         offsets = held.tile([P, TEXTS * TOKENS // 16], U16, name="offsets")
         table = [held.tile([P, VOCAB], F32, name=f"table{d}") for d in range(BLOCKS)]
@@ -40,16 +42,22 @@ def tile_neuronsv2textclassifier_b_kernel(tc, emb, coh, w1, fw1, b1, w2, fw2, b2
         mask = [held.tile([P, TOKENS], BF16, name=f"mask{s}") for s in range(BLOCKS)]
         bias1 = held.tile([P, BLOCKS], F32, name="bias1")
         bias2 = held.tile([P, BLOCKS], F32, name="bias2")
-        picked = [[held.tile([P, TOKENS], F32, name=f"picked{r}_{d}") for d in range(BLOCKS)] for r in range(TEXTS)]
-        x = [[held.tile([P, TOKENS], BF16, name=f"x{r}_{d}") for d in range(BLOCKS)] for r in range(TEXTS)]
+        picked = [
+            [[held.tile([P, PIECE], F32, name=f"picked{r}_{d}_{i}") for i in range(PIECES)] for d in range(BLOCKS)]
+            for r in range(TEXTS)
+        ]
+        x = [
+            [[held.tile([P, PIECE], BF16, name=f"x{r}_{d}_{i}") for i in range(PIECES)] for d in range(BLOCKS)]
+            for r in range(TEXTS)
+        ]
         y = [[held.tile([P, FEATURES], BF16, name=f"y{r}_{s}") for s in range(BLOCKS)] for r in range(TEXTS)]
         h = [[held.tile([P, TOKENS], BF16, name=f"h{r}_{m}") for m in range(BLOCKS)] for r in range(TEXTS)]
         result = [[held.tile([P, TOKENS], F32, name=f"result{r}_{e}") for e in range(BLOCKS)] for r in range(TEXTS)]
 
         zeros = held.tile([P, 1], F32, name="zeros")
-        unused = held.tile([P, 1], F32, name="unused")
+        discarded = held.tile([P, 1], F32, name="discarded")
         nc.vector.memset(zeros[:], 0.0)
-        nc.scalar.activation(unused[:], zeros[:], SIGMOID)
+        nc.scalar.activation(discarded[:], zeros[:], SIGMOID)
 
         nc.sync.dma_start(offsets[:], offs)
         for d in range(BLOCKS):
@@ -67,21 +75,24 @@ def tile_neuronsv2textclassifier_b_kernel(tc, emb, coh, w1, fw1, b1, w2, fw2, b2
             nc.gpsimd.dma_start(bias2[:], b2.rearrange("(e p) o -> p (e o)", p=P))
 
         def look_up(r, d):
-            for first in range(0, TOKENS, PIECE):
-                column = (r * TOKENS + first) // 16
+            for i in range(PIECES):
+                first = (r * TOKENS + i * PIECE) // 16
                 nc.scalar.activation(
-                    picked[r][d][:, first : first + PIECE],
-                    table[d][:].indirect(offsets[:, column : column + PIECE // 16]),
-                    COPY,
+                    picked[r][d][i][:], table[d][:].indirect(offsets[:, first : first + PIECE // 16]), COPY
                 )
-            nc.gpsimd.tensor_copy(x[r][d][:], picked[r][d][:])
+                nc.gpsimd.tensor_copy(x[r][d][i][:], picked[r][d][i][:])
 
         def step_a(r):
             banks = [psum.tile([P, FEATURES], F32, name="bank") for s in range(BLOCKS)]
             for d in range(BLOCKS):
                 for s in range(BLOCKS):
+                    i, within = divmod(s * P, PIECE)
                     nc.tensor.matmul(
-                        banks[s][:], x[r][d][:, block(s)], weights1[d][:], start=(d == 0), stop=(d == BLOCKS - 1)
+                        banks[s][:],
+                        x[r][d][i][:, within : within + P],
+                        weights1[d][:],
+                        start=(d == 0),
+                        stop=(d == BLOCKS - 1),
                     )
             for s in range(BLOCKS):
                 nc.vector.tensor_copy(y[r][s][:], banks[s][:])
@@ -96,13 +107,22 @@ def tile_neuronsv2textclassifier_b_kernel(tc, emb, coh, w1, fw1, b1, w2, fw2, b2
             for m in range(BLOCKS):
                 nc.scalar.activation(h[r][m][:], banks[m][:], TANH, bias=bias1[:, m : m + 1], scale=1.0 / TOKENS)
 
-        def step_c(r):
+        def step_c(r, width):
             for e in range(BLOCKS):
-                bank = psum.tile([P, TOKENS], F32, name="bank")
-                for m in range(BLOCKS):
-                    nc.tensor.matmul(bank[:], weights2[m][:, block(e)], h[r][m][:], start=(m == 0), stop=(m == BLOCKS - 1))
-                nc.scalar.activation(result[r][e][:], bank[:], TANH, bias=bias2[:, e : e + 1])
-                nc.sync.dma_start(out[block(e), r * TOKENS : (r + 1) * TOKENS], result[r][e][:])
+                for t in range(0, TOKENS, width):
+                    bank = psum.tile([P, width], F32, name="bank")
+                    for m in range(BLOCKS):
+                        nc.tensor.matmul(
+                            bank[:],
+                            weights2[m][:, block(e)],
+                            h[r][m][:, t : t + width],
+                            start=(m == 0),
+                            stop=(m == BLOCKS - 1),
+                        )
+                    nc.scalar.activation(result[r][e][:, t : t + width], bank[:], TANH, bias=bias2[:, e : e + 1])
+                    nc.sync.dma_start(
+                        out[block(e), r * TOKENS + t : r * TOKENS + t + width], result[r][e][:, t : t + width]
+                    )
 
         for d in range(BLOCKS):
             nc.vector.tensor_tensor(weights1[d][:], slow1[d][:], fast1[d][:], ADD)
@@ -117,5 +137,5 @@ def tile_neuronsv2textclassifier_b_kernel(tc, emb, coh, w1, fw1, b1, w2, fw2, b2
         step_b(0)
         for r in range(1, TEXTS):
             step_b(r)
-            step_c(r - 1)
-        step_c(TEXTS - 1)
+            step_c(r - 1, TOKENS)
+        step_c(TEXTS - 1, TOKENS // 2)

@@ -28,6 +28,7 @@ def tile_neuronsv2textclassifier_b_kernel(tc, emb, coh, w1, fw1, b1, w2, fw2, b2
     nc = tc.nc
     with (
         tc.tile_pool(name="held", bufs=1) as held,
+        tc.tile_pool(name="twice", bufs=1) as twice,
         tc.psum_pool(name="psum", bufs=PSUM_BANKS) as psum,
     ):
         offsets = held.tile([P, TEXTS * TOKENS // 16], U16, name="offsets")
@@ -38,13 +39,13 @@ def tile_neuronsv2textclassifier_b_kernel(tc, emb, coh, w1, fw1, b1, w2, fw2, b2
         fast2 = [held.tile([P, FEATURES], F32, name=f"fast2_{m}") for m in range(BLOCKS)]
         weights1 = [held.tile([P, FEATURES], BF16, name=f"weights1_{d}") for d in range(BLOCKS)]
         weights2 = [held.tile([P, FEATURES], BF16, name=f"weights2_{m}") for m in range(BLOCKS)]
-        coherence = [held.tile([P, TOKENS], F32, name=f"coherence{s}") for s in range(BLOCKS)]
+        coherence = twice.tile([P, BLOCKS * TOKENS], F32, name="coherence", tag="coh_then_picked")
         mask = [held.tile([P, TOKENS], BF16, name=f"mask{s}") for s in range(BLOCKS)]
         bias1 = held.tile([P, BLOCKS], F32, name="bias1")
         bias2 = held.tile([P, BLOCKS], F32, name="bias2")
         picked = [
-            [[held.tile([P, PIECE], F32, name=f"picked{r}_{d}_{i}") for i in range(PIECES)] for d in range(BLOCKS)]
-            for r in range(TEXTS)
+            [[held.tile([P, PIECE], F32, name=f"picked{r}_{d}_{i}")[:] for i in range(PIECES)] for d in range(BLOCKS)]
+            for r in range(TEXTS - 1)
         ]
         x = [
             [[held.tile([P, PIECE], BF16, name=f"x{r}_{d}_{i}") for i in range(PIECES)] for d in range(BLOCKS)]
@@ -66,7 +67,7 @@ def tile_neuronsv2textclassifier_b_kernel(tc, emb, coh, w1, fw1, b1, w2, fw2, b2
             nc.sync.dma_start(slow1[d][:], w1[block(d), :])
             nc.sync.dma_start(fast1[d][:], fw1[block(d), :])
         for s in range(BLOCKS):
-            nc.sync.dma_start(coherence[s][:], coh[block(s), :])
+            nc.sync.dma_start(coherence[:, s * TOKENS : (s + 1) * TOKENS], coh[block(s), :])
         for m in range(BLOCKS):
             nc.sync.dma_start(slow2[m][:], w2[block(m), :])
             nc.sync.dma_start(fast2[m][:], fw2[block(m), :])
@@ -78,9 +79,9 @@ def tile_neuronsv2textclassifier_b_kernel(tc, emb, coh, w1, fw1, b1, w2, fw2, b2
             for i in range(PIECES):
                 first = (r * TOKENS + i * PIECE) // 16
                 nc.scalar.activation(
-                    picked[r][d][i][:], table[d][:].indirect(offsets[:, first : first + PIECE // 16]), COPY
+                    picked[r][d][i], table[d][:].indirect(offsets[:, first : first + PIECE // 16]), COPY
                 )
-                nc.gpsimd.tensor_copy(x[r][d][i][:], picked[r][d][i][:])
+                nc.gpsimd.tensor_copy(x[r][d][i][:], picked[r][d][i])
 
         def step_a(r):
             banks = [psum.tile([P, FEATURES], F32, name="bank") for s in range(BLOCKS)]
@@ -126,15 +127,25 @@ def tile_neuronsv2textclassifier_b_kernel(tc, emb, coh, w1, fw1, b1, w2, fw2, b2
 
         for d in range(BLOCKS):
             nc.vector.tensor_tensor(weights1[d][:], slow1[d][:], fast1[d][:], ADD)
-        for r in range(TEXTS):
+        for r in range(TEXTS - 1):
             for d in range(BLOCKS):
                 look_up(r, d)
             step_a(r)
         for s in range(BLOCKS):
-            nc.scalar.activation(mask[s][:], coherence[s][:], SIGMOID)
+            nc.scalar.activation(mask[s][:], coherence[:, s * TOKENS : (s + 1) * TOKENS], SIGMOID)
         for m in range(BLOCKS):
             nc.vector.tensor_tensor(weights2[m][:], slow2[m][:], fast2[m][:], ADD)
         step_b(0)
+        last_picked = twice.tile([P, BLOCKS * TOKENS], F32, name="last_picked", tag="coh_then_picked")
+        picked.append(
+            [
+                [last_picked[:, (d * PIECES + i) * PIECE : (d * PIECES + i + 1) * PIECE] for i in range(PIECES)]
+                for d in range(BLOCKS)
+            ]
+        )
+        for d in range(BLOCKS):
+            look_up(TEXTS - 1, d)
+        step_a(TEXTS - 1)
         for r in range(1, TEXTS):
             step_b(r)
             step_c(r - 1, TOKENS)

@@ -16,7 +16,9 @@ TOKENS = 512
 BLOCKS = FEATURES // P
 PIECE = VOCAB
 PIECES = TOKENS // PIECE
-PSUM_BANKS = 8
+BLOCKS_OF_A_PIECE = PIECE // P
+BANKS_OF_A_SIDE = 4
+EARLY_TEXTS = 2
 FLOPS = 3 * 2 * FEATURES * FEATURES * TEXTS * TOKENS
 
 
@@ -28,8 +30,8 @@ def tile_neuronsv2textclassifier_b_kernel(tc, emb, coh, w1, fw1, b1, w2, fw2, b2
     nc = tc.nc
     with (
         tc.tile_pool(name="held", bufs=1) as held,
-        tc.tile_pool(name="twice", bufs=1) as twice,
-        tc.psum_pool(name="psum", bufs=PSUM_BANKS) as psum,
+        tc.tile_pool(name="reused", bufs=1) as reused,
+        tc.psum_pool(name="psum", bufs=BANKS_OF_A_SIDE) as psum,
     ):
         offsets = held.tile([P, TEXTS * TOKENS // 16], U16, name="offsets")
         table = [held.tile([P, VOCAB], F32, name=f"table{d}") for d in range(BLOCKS)]
@@ -39,14 +41,9 @@ def tile_neuronsv2textclassifier_b_kernel(tc, emb, coh, w1, fw1, b1, w2, fw2, b2
         fast2 = [held.tile([P, FEATURES], F32, name=f"fast2_{m}") for m in range(BLOCKS)]
         weights1 = [held.tile([P, FEATURES], BF16, name=f"weights1_{d}") for d in range(BLOCKS)]
         weights2 = [held.tile([P, FEATURES], BF16, name=f"weights2_{m}") for m in range(BLOCKS)]
-        coherence = twice.tile([P, BLOCKS * TOKENS], F32, name="coherence", tag="coh_then_picked")
         mask = [held.tile([P, TOKENS], BF16, name=f"mask{s}") for s in range(BLOCKS)]
         bias1 = held.tile([P, BLOCKS], F32, name="bias1")
         bias2 = held.tile([P, BLOCKS], F32, name="bias2")
-        picked = [
-            [[held.tile([P, PIECE], F32, name=f"picked{r}_{d}_{i}")[:] for i in range(PIECES)] for d in range(BLOCKS)]
-            for r in range(TEXTS - 1)
-        ]
         x = [
             [[held.tile([P, PIECE], BF16, name=f"x{r}_{d}_{i}") for i in range(PIECES)] for d in range(BLOCKS)]
             for r in range(TEXTS)
@@ -55,19 +52,29 @@ def tile_neuronsv2textclassifier_b_kernel(tc, emb, coh, w1, fw1, b1, w2, fw2, b2
         h = [[held.tile([P, TOKENS], BF16, name=f"h{r}_{m}") for m in range(BLOCKS)] for r in range(TEXTS)]
         result = [[held.tile([P, TOKENS], F32, name=f"result{r}_{e}") for e in range(BLOCKS)] for r in range(TEXTS)]
 
+        blocks_of_a_slot = BLOCKS // PIECES
+        coherence = [
+            reused.tile([P, blocks_of_a_slot * TOKENS], F32, name=f"coherence{i}", tag=f"slot{i}")
+            for i in range(PIECES)
+        ]
+
         zeros = held.tile([P, 1], F32, name="zeros")
         discarded = held.tile([P, 1], F32, name="discarded")
         nc.vector.memset(zeros[:], 0.0)
         nc.scalar.activation(discarded[:], zeros[:], SIGMOID)
 
         nc.sync.dma_start(offsets[:], offs)
-        for d in range(BLOCKS):
+        nc.sync.dma_start(table[0][:], emb[block(0), :])
+        nc.sync.dma_start(slow1[0][:], w1[block(0), :])
+        nc.sync.dma_start(fast1[0][:], fw1[block(0), :])
+        for d in range(1, BLOCKS):
             nc.sync.dma_start(table[d][:], emb[block(d), :])
-        for d in range(BLOCKS):
+        for d in range(1, BLOCKS):
             nc.sync.dma_start(slow1[d][:], w1[block(d), :])
             nc.sync.dma_start(fast1[d][:], fw1[block(d), :])
         for s in range(BLOCKS):
-            nc.sync.dma_start(coherence[:, s * TOKENS : (s + 1) * TOKENS], coh[block(s), :])
+            i, k = divmod(s, blocks_of_a_slot)
+            nc.sync.dma_start(coherence[i][:, k * TOKENS : (k + 1) * TOKENS], coh[block(s), :])
         for m in range(BLOCKS):
             nc.sync.dma_start(slow2[m][:], w2[block(m), :])
             nc.sync.dma_start(fast2[m][:], fw2[block(m), :])
@@ -75,31 +82,25 @@ def tile_neuronsv2textclassifier_b_kernel(tc, emb, coh, w1, fw1, b1, w2, fw2, b2
             nc.gpsimd.dma_start(bias1[:], b1.rearrange("(m p) o -> p (m o)", p=P))
             nc.gpsimd.dma_start(bias2[:], b2.rearrange("(e p) o -> p (e o)", p=P))
 
-        def look_up(r, d):
-            for i in range(PIECES):
-                first = (r * TOKENS + i * PIECE) // 16
-                nc.scalar.activation(
-                    picked[r][d][i], table[d][:].indirect(offsets[:, first : first + PIECE // 16]), COPY
-                )
-                nc.gpsimd.tensor_copy(x[r][d][i][:], picked[r][d][i])
+        def look_up(r, d, i, picked):
+            first = (r * TOKENS + i * PIECE) // 16
+            nc.scalar.activation(picked, table[d][:].indirect(offsets[:, first : first + PIECE // 16]), COPY)
+            nc.gpsimd.tensor_copy(x[r][d][i][:], picked)
 
-        def step_a(r):
-            banks = [psum.tile([P, FEATURES], F32, name="bank") for s in range(BLOCKS)]
+        def step_a(r, pieces, side):
+            blocks_of_tokens = [i * BLOCKS_OF_A_PIECE + k for i in pieces for k in range(BLOCKS_OF_A_PIECE)]
+            banks = {s: psum.tile([P, FEATURES], F32, name="bank", tag=side) for s in blocks_of_tokens}
             for d in range(BLOCKS):
-                for s in range(BLOCKS):
-                    i, within = divmod(s * P, PIECE)
+                for s in blocks_of_tokens:
+                    i, k = divmod(s, BLOCKS_OF_A_PIECE)
                     nc.tensor.matmul(
-                        banks[s][:],
-                        x[r][d][i][:, within : within + P],
-                        weights1[d][:],
-                        start=(d == 0),
-                        stop=(d == BLOCKS - 1),
+                        banks[s][:], x[r][d][i][:, block(k)], weights1[d][:], start=(d == 0), stop=(d == BLOCKS - 1)
                     )
-            for s in range(BLOCKS):
+            for s in blocks_of_tokens:
                 nc.vector.tensor_copy(y[r][s][:], banks[s][:])
 
         def step_b(r):
-            banks = [psum.tile([P, TOKENS], F32, name="bank") for m in range(BLOCKS)]
+            banks = [psum.tile([P, TOKENS], F32, name="bank", tag="left") for m in range(BLOCKS)]
             for s in range(BLOCKS):
                 for m in range(BLOCKS):
                     nc.tensor.matmul(
@@ -111,7 +112,7 @@ def tile_neuronsv2textclassifier_b_kernel(tc, emb, coh, w1, fw1, b1, w2, fw2, b2
         def step_c(r, width):
             for e in range(BLOCKS):
                 for t in range(0, TOKENS, width):
-                    bank = psum.tile([P, width], F32, name="bank")
+                    bank = psum.tile([P, width], F32, name="bank", tag="right")
                     for m in range(BLOCKS):
                         nc.tensor.matmul(
                             bank[:],
@@ -127,25 +128,23 @@ def tile_neuronsv2textclassifier_b_kernel(tc, emb, coh, w1, fw1, b1, w2, fw2, b2
 
         for d in range(BLOCKS):
             nc.vector.tensor_tensor(weights1[d][:], slow1[d][:], fast1[d][:], ADD)
-        for r in range(TEXTS - 1):
+        for r in range(EARLY_TEXTS):
             for d in range(BLOCKS):
-                look_up(r, d)
-            step_a(r)
+                for i in range(PIECES):
+                    look_up(r, d, i, held.tile([P, PIECE], F32, name=f"picked{r}_{d}_{i}")[:])
+            step_a(r, range(PIECES), ("left", "right")[r])
         for s in range(BLOCKS):
-            nc.scalar.activation(mask[s][:], coherence[:, s * TOKENS : (s + 1) * TOKENS], SIGMOID)
+            i, k = divmod(s, blocks_of_a_slot)
+            nc.scalar.activation(mask[s][:], coherence[i][:, k * TOKENS : (k + 1) * TOKENS], SIGMOID)
+        step_b(0)
         for m in range(BLOCKS):
             nc.vector.tensor_tensor(weights2[m][:], slow2[m][:], fast2[m][:], ADD)
-        step_b(0)
-        last_picked = twice.tile([P, BLOCKS * TOKENS], F32, name="last_picked", tag="coh_then_picked")
-        picked.append(
-            [
-                [last_picked[:, (d * PIECES + i) * PIECE : (d * PIECES + i + 1) * PIECE] for i in range(PIECES)]
-                for d in range(BLOCKS)
-            ]
-        )
-        for d in range(BLOCKS):
-            look_up(TEXTS - 1, d)
-        step_a(TEXTS - 1)
+        for r in range(EARLY_TEXTS, TEXTS):
+            for i in range(PIECES):
+                picked = reused.tile([P, BLOCKS * PIECE], F32, name=f"picked{r}_{i}", tag=f"slot{i}")
+                for d in range(BLOCKS):
+                    look_up(r, d, i, picked[:, d * PIECE : (d + 1) * PIECE])
+                step_a(r, [i], "right")
         for r in range(1, TEXTS):
             step_b(r)
             step_c(r - 1, TOKENS)

@@ -79,8 +79,8 @@ def tile_neuronsv2textclassifier_b_kernel(tc, emb, coh, w1, fw1, b1, w2, fw2, b2
             nc.sync.dma_start(slow2[m][:], w2[block(m), :])
             nc.sync.dma_start(fast2[m][:], fw2[block(m), :])
         with nc.allow_non_contiguous_dma(reason="512 biases, one to a partition, four columns"):
-            nc.gpsimd.dma_start(bias1[:], b1.rearrange("(m p) o -> p (m o)", p=P))
-            nc.gpsimd.dma_start(bias2[:], b2.rearrange("(e p) o -> p (e o)", p=P))
+            nc.sync.dma_start(bias1[:], b1.rearrange("(m p) o -> p (m o)", p=P))
+            nc.sync.dma_start(bias2[:], b2.rearrange("(e p) o -> p (e o)", p=P))
 
         def look_up(r, d, i, picked):
             first = (r * TOKENS + i * PIECE) // 16

@@ -18,7 +18,8 @@ PIECE = VOCAB
 PIECES = TOKENS // PIECE
 BLOCKS_OF_A_PIECE = PIECE // P
 BANKS_OF_A_SIDE = 4
-EARLY_TEXTS = 2
+EARLY_PIECES = [(0, 0), (0, 1), (1, 0)]
+LATE_PIECES = [(1, 1), (2, 0), (2, 1), (3, 0), (3, 1)]
 FLOPS = 3 * 2 * FEATURES * FEATURES * TEXTS * TOKENS
 
 
@@ -69,7 +70,6 @@ def tile_neuronsv2textclassifier_b_kernel(tc, emb, coh, w1, fw1, b1, w2, fw2, b2
         nc.sync.dma_start(fast1[0][:], fw1[block(0), :])
         for d in range(1, BLOCKS):
             nc.sync.dma_start(table[d][:], emb[block(d), :])
-        for d in range(1, BLOCKS):
             nc.sync.dma_start(slow1[d][:], w1[block(d), :])
             nc.sync.dma_start(fast1[d][:], fw1[block(d), :])
         for s in range(BLOCKS):
@@ -87,32 +87,40 @@ def tile_neuronsv2textclassifier_b_kernel(tc, emb, coh, w1, fw1, b1, w2, fw2, b2
             nc.scalar.activation(picked, table[d][:].indirect(offsets[:, first : first + PIECE // 16]), COPY)
             nc.gpsimd.tensor_copy(x[r][d][i][:], picked)
 
-        def step_a(r, pieces, side):
-            blocks_of_tokens = [i * BLOCKS_OF_A_PIECE + k for i in pieces for k in range(BLOCKS_OF_A_PIECE)]
-            banks = {s: psum.tile([P, FEATURES], F32, name="bank", tag=side) for s in blocks_of_tokens}
+        def step_a(pieces):
+            token_blocks = [(r, i, k) for r, i in pieces for k in range(BLOCKS_OF_A_PIECE)]
+            banks = [psum.tile([P, FEATURES], F32, name="bank", tag="right" if r else "left") for r, i, k in token_blocks]
             for d in range(BLOCKS):
-                for s in blocks_of_tokens:
-                    i, k = divmod(s, BLOCKS_OF_A_PIECE)
+                for bank, (r, i, k) in zip(banks, token_blocks):
                     nc.tensor.matmul(
-                        banks[s][:], x[r][d][i][:, block(k)], weights1[d][:], start=(d == 0), stop=(d == BLOCKS - 1)
+                        bank[:], x[r][d][i][:, block(k)], weights1[d][:], start=(d == 0), stop=(d == BLOCKS - 1)
                     )
-            for s in blocks_of_tokens:
-                nc.vector.tensor_copy(y[r][s][:], banks[s][:])
+            for bank, (r, i, k) in zip(banks, token_blocks):
+                nc.vector.tensor_copy(y[r][i * BLOCKS_OF_A_PIECE + k][:], bank[:])
 
-        def step_b(r):
+        def first_step_b():
             banks = [psum.tile([P, TOKENS], F32, name="bank", tag="left") for m in range(BLOCKS)]
             for s in range(BLOCKS):
                 for m in range(BLOCKS):
                     nc.tensor.matmul(
-                        banks[m][:], y[r][s][:, block(m)], mask[s][:], start=(s == 0), stop=(s == BLOCKS - 1)
+                        banks[m][:], y[0][s][:, block(m)], mask[s][:], start=(s == 0), stop=(s == BLOCKS - 1)
                     )
             for m in range(BLOCKS):
-                nc.scalar.activation(h[r][m][:], banks[m][:], TANH, bias=bias1[:, m : m + 1], scale=1.0 / TOKENS)
+                nc.scalar.activation(h[0][m][:], banks[m][:], TANH, bias=bias1[:, m : m + 1], scale=1.0 / TOKENS)
+
+        def step_b(r):
+            for m in range(BLOCKS):
+                bank = psum.tile([P, TOKENS], F32, name="bank", tag="right")
+                for s in range(BLOCKS):
+                    nc.tensor.matmul(
+                        bank[:], y[r][s][:, block(m)], mask[s][:], start=(s == 0), stop=(s == BLOCKS - 1)
+                    )
+                nc.scalar.activation(h[r][m][:], bank[:], TANH, bias=bias1[:, m : m + 1], scale=1.0 / TOKENS)
 
         def step_c(r, width):
             for e in range(BLOCKS):
                 for t in range(0, TOKENS, width):
-                    bank = psum.tile([P, width], F32, name="bank", tag="right")
+                    bank = psum.tile([P, width], F32, name="bank", tag="left")
                     for m in range(BLOCKS):
                         nc.tensor.matmul(
                             bank[:],
@@ -128,23 +136,21 @@ def tile_neuronsv2textclassifier_b_kernel(tc, emb, coh, w1, fw1, b1, w2, fw2, b2
 
         for d in range(BLOCKS):
             nc.vector.tensor_tensor(weights1[d][:], slow1[d][:], fast1[d][:], ADD)
-        for r in range(EARLY_TEXTS):
-            for d in range(BLOCKS):
-                for i in range(PIECES):
-                    look_up(r, d, i, held.tile([P, PIECE], F32, name=f"picked{r}_{d}_{i}")[:])
-            step_a(r, range(PIECES), ("left", "right")[r])
+        for d in range(BLOCKS):
+            for r, i in EARLY_PIECES:
+                look_up(r, d, i, held.tile([P, PIECE], F32, name=f"picked{r}_{d}_{i}")[:])
+        step_a(EARLY_PIECES)
         for s in range(BLOCKS):
             i, k = divmod(s, blocks_of_a_slot)
             nc.scalar.activation(mask[s][:], coherence[i][:, k * TOKENS : (k + 1) * TOKENS], SIGMOID)
-        step_b(0)
+        first_step_b()
         for m in range(BLOCKS):
             nc.vector.tensor_tensor(weights2[m][:], slow2[m][:], fast2[m][:], ADD)
-        for r in range(EARLY_TEXTS, TEXTS):
-            for i in range(PIECES):
-                picked = reused.tile([P, BLOCKS * PIECE], F32, name=f"picked{r}_{i}", tag=f"slot{i}")
-                for d in range(BLOCKS):
-                    look_up(r, d, i, picked[:, d * PIECE : (d + 1) * PIECE])
-                step_a(r, [i], "right")
+        for n, (r, i) in enumerate(LATE_PIECES):
+            picked = reused.tile([P, BLOCKS * PIECE], F32, name=f"picked{r}_{i}", tag=f"slot{n % PIECES}")
+            for d in range(BLOCKS):
+                look_up(r, d, i, picked[:, d * PIECE : (d + 1) * PIECE])
+            step_a([(r, i)])
         for r in range(1, TEXTS):
             step_b(r)
             step_c(r - 1, TOKENS)

@@ -18,6 +18,7 @@ PIECE = VOCAB
 PIECES = TOKENS // PIECE
 BLOCKS_OF_A_PIECE = PIECE // P
 BANKS_OF_A_SIDE = 4
+FIRST_PARTS = 2
 EARLY_PIECES = [(0, 0), (0, 1), (1, 0)]
 LATE_PIECES = [(1, 1), (2, 0), (2, 1), (3, 0), (3, 1)]
 FLOPS = 3 * 2 * FEATURES * FEATURES * TEXTS * TOKENS
@@ -25,6 +26,10 @@ FLOPS = 3 * 2 * FEATURES * FEATURES * TEXTS * TOKENS
 
 def block(i):
     return slice(i * P, (i + 1) * P)
+
+
+def column_parts(columns, parts):
+    return [slice(n * columns // parts, (n + 1) * columns // parts) for n in range(parts)]
 
 
 def tile_neuronsv2textclassifier_b_kernel(tc, emb, coh, w1, fw1, b1, w2, fw2, b2, offs, out):
@@ -66,8 +71,9 @@ def tile_neuronsv2textclassifier_b_kernel(tc, emb, coh, w1, fw1, b1, w2, fw2, b2
 
         nc.sync.dma_start(offsets[:], offs)
         nc.sync.dma_start(table[0][:], emb[block(0), :])
-        nc.sync.dma_start(slow1[0][:], w1[block(0), :])
-        nc.sync.dma_start(fast1[0][:], fw1[block(0), :])
+        for c in column_parts(FEATURES, FIRST_PARTS):
+            nc.sync.dma_start(slow1[0][:, c], w1[block(0), c])
+            nc.sync.dma_start(fast1[0][:, c], fw1[block(0), c])
         for d in range(1, BLOCKS):
             nc.sync.dma_start(table[d][:], emb[block(d), :])
             nc.sync.dma_start(slow1[d][:], w1[block(d), :])
@@ -83,30 +89,39 @@ def tile_neuronsv2textclassifier_b_kernel(tc, emb, coh, w1, fw1, b1, w2, fw2, b2
             nc.sync.dma_start(bias2[:], b2.rearrange("(e p) o -> p (e o)", p=P))
 
         def look_up(r, d, i, picked):
-            first = (r * TOKENS + i * PIECE) // 16
-            nc.scalar.activation(picked, table[d][:].indirect(offsets[:, first : first + PIECE // 16]), COPY)
-            nc.gpsimd.tensor_copy(x[r][d][i][:], picked)
+            for part in column_parts(PIECE, FIRST_PARTS if (r, d, i) == (0, 0, 0) else 1):
+                first, last = [(r * TOKENS + i * PIECE + t) // 16 for t in (part.start, part.stop)]
+                nc.scalar.activation(picked[:, part], table[d][:].indirect(offsets[:, first:last]), COPY)
+                nc.gpsimd.tensor_copy(x[r][d][i][:, part], picked[:, part])
 
         def step_a(pieces):
             token_blocks = [(r, i, k) for r, i in pieces for k in range(BLOCKS_OF_A_PIECE)]
             banks = [psum.tile([P, FEATURES], F32, name="bank", tag="right" if r else "left") for r, i, k in token_blocks]
+            bank_of = dict(zip(token_blocks, banks))
             for d in range(BLOCKS):
-                for bank, (r, i, k) in zip(banks, token_blocks):
-                    nc.tensor.matmul(
-                        bank[:], x[r][d][i][:, block(k)], weights1[d][:], start=(d == 0), stop=(d == BLOCKS - 1)
-                    )
-            for bank, (r, i, k) in zip(banks, token_blocks):
-                nc.vector.tensor_copy(y[r][i * BLOCKS_OF_A_PIECE + k][:], bank[:])
+                for r, i in pieces:
+                    for c in column_parts(FEATURES, FIRST_PARTS if (r, d, i) == (0, 0, 0) else 1):
+                        for k in range(BLOCKS_OF_A_PIECE):
+                            nc.tensor.matmul(
+                                bank_of[r, i, k][:, c],
+                                x[r][d][i][:, block(k)],
+                                weights1[d][:, c],
+                                start=(d == 0 and c.start == 0),
+                                stop=(d == BLOCKS - 1),
+                            )
+            for r, i, k in token_blocks:
+                nc.vector.tensor_copy(y[r][i * BLOCKS_OF_A_PIECE + k][:], bank_of[r, i, k][:])
 
         def first_step_b():
-            banks = [psum.tile([P, TOKENS], F32, name="bank", tag="left") for m in range(BLOCKS)]
-            for s in range(BLOCKS):
-                for m in range(BLOCKS):
-                    nc.tensor.matmul(
-                        banks[m][:], y[0][s][:, block(m)], mask[s][:], start=(s == 0), stop=(s == BLOCKS - 1)
-                    )
-            for m in range(BLOCKS):
-                nc.scalar.activation(h[0][m][:], banks[m][:], TANH, bias=bias1[:, m : m + 1], scale=1.0 / TOKENS)
+            for pair in range(0, BLOCKS, 2):
+                banks = {m: psum.tile([P, TOKENS], F32, name="bank", tag="left") for m in (pair, pair + 1)}
+                for s in range(BLOCKS):
+                    for m, bank in banks.items():
+                        nc.tensor.matmul(
+                            bank[:], y[0][s][:, block(m)], mask[s][:], start=(s == 0), stop=(s == BLOCKS - 1)
+                        )
+                for m, bank in banks.items():
+                    nc.scalar.activation(h[0][m][:], bank[:], TANH, bias=bias1[:, m : m + 1], scale=1.0 / TOKENS)
 
         def step_b(r):
             for m in range(BLOCKS):
@@ -135,7 +150,8 @@ def tile_neuronsv2textclassifier_b_kernel(tc, emb, coh, w1, fw1, b1, w2, fw2, b2
                     )
 
         for d in range(BLOCKS):
-            nc.vector.tensor_tensor(weights1[d][:], slow1[d][:], fast1[d][:], ADD)
+            for c in column_parts(FEATURES, FIRST_PARTS if d == 0 else 1):
+                nc.vector.tensor_tensor(weights1[d][:, c], slow1[d][:, c], fast1[d][:, c], ADD)
         for d in range(BLOCKS):
             for r, i in EARLY_PIECES:
                 look_up(r, d, i, held.tile([P, PIECE], F32, name=f"picked{r}_{d}_{i}")[:])

@@ -17,10 +17,13 @@ BLOCKS = FEATURES // P
 PIECE = VOCAB
 PIECES = TOKENS // PIECE
 BLOCKS_OF_A_PIECE = PIECE // P
+SIDE_OF_STEP_A = ("left", "right", "right", "left")
 BANKS_OF_A_SIDE = 4
+LAST_PARTS = 2
 FIRST_PARTS = 2
 EARLY_PIECES = [(0, 0), (0, 1), (1, 0)]
-LATE_PIECES = [(1, 1), (2, 0), (2, 1), (3, 0), (3, 1)]
+MIDDLE_PIECES = [(1, 1), (2, 0), (2, 1)]
+LAST_PIECES = [(3, 0), (3, 1)]
 FLOPS = 3 * 2 * FEATURES * FEATURES * TEXTS * TOKENS
 
 
@@ -54,15 +57,16 @@ def tile_neuronsv2textclassifier_b_kernel(tc, emb, coh, w1, fw1, b1, w2, fw2, b2
             [[held.tile([P, PIECE], BF16, name=f"x{r}_{d}_{i}") for i in range(PIECES)] for d in range(BLOCKS)]
             for r in range(TEXTS)
         ]
-        y = [[held.tile([P, FEATURES], BF16, name=f"y{r}_{s}") for s in range(BLOCKS)] for r in range(TEXTS)]
+        y = [None] + [[held.tile([P, FEATURES], BF16, name=f"y{r}_{s}") for s in range(BLOCKS)] for r in range(1, TEXTS)]
         h = [[held.tile([P, TOKENS], BF16, name=f"h{r}_{m}") for m in range(BLOCKS)] for r in range(TEXTS)]
         result = [[held.tile([P, TOKENS], F32, name=f"result{r}_{e}") for e in range(BLOCKS)] for r in range(TEXTS)]
 
         blocks_of_a_slot = BLOCKS // PIECES
         coherence = [
-            reused.tile([P, blocks_of_a_slot * TOKENS], F32, name=f"coherence{i}", tag=f"slot{i}")
+            reused.tile([P, blocks_of_a_slot * TOKENS], F32, name=f"coherence{i}", tag=f"coh{i}")
             for i in range(PIECES)
         ]
+        y[0] = [reused.tile([P, FEATURES], BF16, name=f"y0_{s}", tag=f"y{s}") for s in range(BLOCKS)]
 
         zeros = held.tile([P, 1], F32, name="zeros")
         discarded = held.tile([P, 1], F32, name="discarded")
@@ -96,7 +100,7 @@ def tile_neuronsv2textclassifier_b_kernel(tc, emb, coh, w1, fw1, b1, w2, fw2, b2
 
         def step_a(pieces):
             token_blocks = [(r, i, k) for r, i in pieces for k in range(BLOCKS_OF_A_PIECE)]
-            banks = [psum.tile([P, FEATURES], F32, name="bank", tag="right" if r else "left") for r, i, k in token_blocks]
+            banks = [psum.tile([P, FEATURES], F32, name="bank", tag=SIDE_OF_STEP_A[r]) for r, i, k in token_blocks]
             bank_of = dict(zip(token_blocks, banks))
             for d in range(BLOCKS):
                 for r, i in pieces:
@@ -132,22 +136,21 @@ def tile_neuronsv2textclassifier_b_kernel(tc, emb, coh, w1, fw1, b1, w2, fw2, b2
                     )
                 nc.scalar.activation(h[r][m][:], bank[:], TANH, bias=bias1[:, m : m + 1], scale=1.0 / TOKENS)
 
-        def step_c(r, width):
+        def step_c(r):
             for e in range(BLOCKS):
-                for t in range(0, TOKENS, width):
-                    bank = psum.tile([P, width], F32, name="bank", tag="left")
+                parts = LAST_PARTS if (r, e) == (TEXTS - 1, BLOCKS - 1) else 1
+                for c in column_parts(TOKENS, parts):
+                    bank = psum.tile([P, TOKENS // parts], F32, name="bank", tag="left")
                     for m in range(BLOCKS):
                         nc.tensor.matmul(
-                            bank[:],
-                            weights2[m][:, block(e)],
-                            h[r][m][:, t : t + width],
-                            start=(m == 0),
-                            stop=(m == BLOCKS - 1),
+                            bank[:], weights2[m][:, block(e)], h[r][m][:, c], start=(m == 0), stop=(m == BLOCKS - 1)
                         )
-                    nc.scalar.activation(result[r][e][:, t : t + width], bank[:], TANH, bias=bias2[:, e : e + 1])
-                    nc.sync.dma_start(
-                        out[block(e), r * TOKENS + t : r * TOKENS + t + width], result[r][e][:, t : t + width]
-                    )
+                    for q in column_parts(TOKENS // parts, parts):
+                        t = slice(c.start + q.start, c.start + q.stop)
+                        nc.scalar.activation(result[r][e][:, t], bank[:, q], TANH, bias=bias2[:, e : e + 1])
+                        nc.sync.dma_start(
+                            out[block(e), r * TOKENS + t.start : r * TOKENS + t.stop], result[r][e][:, t]
+                        )
 
         for d in range(BLOCKS):
             for c in column_parts(FEATURES, FIRST_PARTS if d == 0 else 1):
@@ -162,12 +165,18 @@ def tile_neuronsv2textclassifier_b_kernel(tc, emb, coh, w1, fw1, b1, w2, fw2, b2
         first_step_b()
         for m in range(BLOCKS):
             nc.vector.tensor_tensor(weights2[m][:], slow2[m][:], fast2[m][:], ADD)
-        for n, (r, i) in enumerate(LATE_PIECES):
-            picked = reused.tile([P, BLOCKS * PIECE], F32, name=f"picked{r}_{i}", tag=f"slot{n % PIECES}")
+        for n, (r, i) in enumerate(MIDDLE_PIECES):
+            picked = reused.tile([P, BLOCKS * PIECE], F32, name=f"picked{r}_{i}", tag=f"coh{n % PIECES}")
             for d in range(BLOCKS):
                 look_up(r, d, i, picked[:, d * PIECE : (d + 1) * PIECE])
             step_a([(r, i)])
-        for r in range(1, TEXTS):
+        step_b(1)
+        for r, i in LAST_PIECES:
+            for d in range(BLOCKS):
+                look_up(r, d, i, reused.tile([P, PIECE], F32, name=f"picked{r}_{d}_{i}", tag=f"y{d}")[:])
+            step_a([(r, i)])
+        step_c(0)
+        for r in range(2, TEXTS):
             step_b(r)
-            step_c(r - 1, TOKENS)
-        step_c(TEXTS - 1, TOKENS // 2)
+            step_c(r - 1)
+        step_c(TEXTS - 1)

@@ -19,7 +19,6 @@ PIECES = TOKENS // PIECE
 BLOCKS_OF_A_PIECE = PIECE // P
 SIDE_OF_STEP_A = ("left", "right", "right", "left")
 BANKS_OF_A_SIDE = 4
-LAST_PARTS = 2
 FIRST_PARTS = 2
 EARLY_PIECES = [(0, 0), (0, 1), (1, 0)]
 MIDDLE_PIECES = [(1, 1), (2, 0), (2, 1)]
@@ -137,20 +136,19 @@ def tile_neuronsv2textclassifier_b_kernel(tc, emb, coh, w1, fw1, b1, w2, fw2, b2
                 nc.scalar.activation(h[r][m][:], bank[:], TANH, bias=bias1[:, m : m + 1], scale=1.0 / TOKENS)
 
         def step_c(r):
+            half, quarter = TOKENS // 2, TOKENS // 4
             for e in range(BLOCKS):
-                parts = LAST_PARTS if (r, e) == (TEXTS - 1, BLOCKS - 1) else 1
-                for c in column_parts(TOKENS, parts):
-                    bank = psum.tile([P, TOKENS // parts], F32, name="bank", tag="left")
+                first = 0
+                for width in (half, quarter, quarter) if (r, e) == (TEXTS - 1, BLOCKS - 1) else (TOKENS,):
+                    t = slice(first, first + width)
+                    bank = psum.tile([P, width], F32, name="bank", tag="left")
                     for m in range(BLOCKS):
                         nc.tensor.matmul(
-                            bank[:], weights2[m][:, block(e)], h[r][m][:, c], start=(m == 0), stop=(m == BLOCKS - 1)
+                            bank[:], weights2[m][:, block(e)], h[r][m][:, t], start=(m == 0), stop=(m == BLOCKS - 1)
                         )
-                    for q in column_parts(TOKENS // parts, parts):
-                        t = slice(c.start + q.start, c.start + q.stop)
-                        nc.scalar.activation(result[r][e][:, t], bank[:, q], TANH, bias=bias2[:, e : e + 1])
-                        nc.sync.dma_start(
-                            out[block(e), r * TOKENS + t.start : r * TOKENS + t.stop], result[r][e][:, t]
-                        )
+                    nc.scalar.activation(result[r][e][:, t], bank[:], TANH, bias=bias2[:, e : e + 1])
+                    nc.sync.dma_start(out[block(e), r * TOKENS + t.start : r * TOKENS + t.stop], result[r][e][:, t])
+                    first += width
 
         for d in range(BLOCKS):
             for c in column_parts(FEATURES, FIRST_PARTS if d == 0 else 1):

import concourse.mybir as mybir

F32 = mybir.dt.float32
BF16 = mybir.dt.bfloat16
U16 = mybir.dt.uint16
COPY = mybir.ActivationFunctionType.Copy
SIGMOID = mybir.ActivationFunctionType.Sigmoid
TANH = mybir.ActivationFunctionType.Tanh
ADD = mybir.AluOpType.add

P = 128
VOCAB = 256
FEATURES = 512
TEXTS = 4
TOKENS = 512
BLOCKS = FEATURES // P
PIECE = VOCAB
PIECES = TOKENS // PIECE
BLOCKS_OF_A_PIECE = PIECE // P
SIDE_OF_STEP_A = ("left", "right", "right", "left")
BANKS_OF_A_SIDE = 4
FIRST_PARTS = 2
EARLY_PIECES = [(0, 0), (0, 1), (1, 0)]
MIDDLE_PIECES = [(1, 1), (2, 0), (2, 1)]
LAST_PIECES = [(3, 0), (3, 1)]
FLOPS = 3 * 2 * FEATURES * FEATURES * TEXTS * TOKENS


def block(i):
    return slice(i * P, (i + 1) * P)


def column_parts(columns, parts):
    return [slice(n * columns // parts, (n + 1) * columns // parts) for n in range(parts)]


def tile_neuronsv2textclassifier_b_kernel(tc, emb, coh, w1, fw1, b1, w2, fw2, b2, offs, out):
    nc = tc.nc
    with (
        tc.tile_pool(name="held", bufs=1) as held,
        tc.tile_pool(name="reused", bufs=1) as reused,
        tc.psum_pool(name="psum", bufs=BANKS_OF_A_SIDE) as psum,
    ):
        offsets = held.tile([P, TEXTS * TOKENS // 16], U16, name="offsets")
        table = [held.tile([P, VOCAB], F32, name=f"table{d}") for d in range(BLOCKS)]
        slow1 = [held.tile([P, FEATURES], F32, name=f"slow1_{d}") for d in range(BLOCKS)]
        fast1 = [held.tile([P, FEATURES], F32, name=f"fast1_{d}") for d in range(BLOCKS)]
        slow2 = [held.tile([P, FEATURES], F32, name=f"slow2_{m}") for m in range(BLOCKS)]
        fast2 = [held.tile([P, FEATURES], F32, name=f"fast2_{m}") for m in range(BLOCKS)]
        weights1 = [held.tile([P, FEATURES], BF16, name=f"weights1_{d}") for d in range(BLOCKS)]
        weights2 = [held.tile([P, FEATURES], BF16, name=f"weights2_{m}") for m in range(BLOCKS)]
        mask = [held.tile([P, TOKENS], BF16, name=f"mask{s}") for s in range(BLOCKS)]
        bias1 = held.tile([P, BLOCKS], F32, name="bias1")
        bias2 = held.tile([P, BLOCKS], F32, name="bias2")
        x = [
            [[held.tile([P, PIECE], BF16, name=f"x{r}_{d}_{i}") for i in range(PIECES)] for d in range(BLOCKS)]
            for r in range(TEXTS)
        ]
        y = [None] + [[held.tile([P, FEATURES], BF16, name=f"y{r}_{s}") for s in range(BLOCKS)] for r in range(1, TEXTS)]
        h = [[held.tile([P, TOKENS], BF16, name=f"h{r}_{m}") for m in range(BLOCKS)] for r in range(TEXTS)]
        result = [[held.tile([P, TOKENS], F32, name=f"result{r}_{e}") for e in range(BLOCKS)] for r in range(TEXTS)]

        blocks_of_a_slot = BLOCKS // PIECES
        coherence = [
            reused.tile([P, blocks_of_a_slot * TOKENS], F32, name=f"coherence{i}", tag=f"coh{i}")
            for i in range(PIECES)
        ]
        y[0] = [reused.tile([P, FEATURES], BF16, name=f"y0_{s}", tag=f"y{s}") for s in range(BLOCKS)]

        zeros = held.tile([P, 1], F32, name="zeros")
        discarded = held.tile([P, 1], F32, name="discarded")
        nc.vector.memset(zeros[:], 0.0)
        nc.scalar.activation(discarded[:], zeros[:], SIGMOID)

        nc.sync.dma_start(offsets[:], offs)
        nc.sync.dma_start(table[0][:], emb[block(0), :])
        for c in column_parts(FEATURES, FIRST_PARTS):
            nc.sync.dma_start(slow1[0][:, c], w1[block(0), c])
            nc.sync.dma_start(fast1[0][:, c], fw1[block(0), c])
        for d in range(1, BLOCKS):
            nc.sync.dma_start(table[d][:], emb[block(d), :])
            nc.sync.dma_start(slow1[d][:], w1[block(d), :])
            nc.sync.dma_start(fast1[d][:], fw1[block(d), :])
        for s in range(BLOCKS):
            i, k = divmod(s, blocks_of_a_slot)
            nc.sync.dma_start(coherence[i][:, k * TOKENS : (k + 1) * TOKENS], coh[block(s), :])
        for m in range(BLOCKS):
            nc.sync.dma_start(slow2[m][:], w2[block(m), :])
            nc.sync.dma_start(fast2[m][:], fw2[block(m), :])
        with nc.allow_non_contiguous_dma(reason="512 biases, one to a partition, four columns"):
            nc.sync.dma_start(bias1[:], b1.rearrange("(m p) o -> p (m o)", p=P))
            nc.sync.dma_start(bias2[:], b2.rearrange("(e p) o -> p (e o)", p=P))

        def look_up(r, d, i, picked):
            for part in column_parts(PIECE, FIRST_PARTS if (r, d, i) == (0, 0, 0) else 1):
                first, last = [(r * TOKENS + i * PIECE + t) // 16 for t in (part.start, part.stop)]
                nc.scalar.activation(picked[:, part], table[d][:].indirect(offsets[:, first:last]), COPY)
                nc.gpsimd.tensor_copy(x[r][d][i][:, part], picked[:, part])

        def step_a(pieces):
            token_blocks = [(r, i, k) for r, i in pieces for k in range(BLOCKS_OF_A_PIECE)]
            banks = [psum.tile([P, FEATURES], F32, name="bank", tag=SIDE_OF_STEP_A[r]) for r, i, k in token_blocks]
            bank_of = dict(zip(token_blocks, banks))
            for d in range(BLOCKS):
                for r, i in pieces:
                    for c in column_parts(FEATURES, FIRST_PARTS if (r, d, i) == (0, 0, 0) else 1):
                        for k in range(BLOCKS_OF_A_PIECE):
                            nc.tensor.matmul(
                                bank_of[r, i, k][:, c],
                                x[r][d][i][:, block(k)],
                                weights1[d][:, c],
                                start=(d == 0 and c.start == 0),
                                stop=(d == BLOCKS - 1),
                            )
            for r, i, k in token_blocks:
                nc.vector.tensor_copy(y[r][i * BLOCKS_OF_A_PIECE + k][:], bank_of[r, i, k][:])

        def first_step_b():
            for pair in range(0, BLOCKS, 2):
                banks = {m: psum.tile([P, TOKENS], F32, name="bank", tag="left") for m in (pair, pair + 1)}
                for s in range(BLOCKS):
                    for m, bank in banks.items():
                        nc.tensor.matmul(
                            bank[:], y[0][s][:, block(m)], mask[s][:], start=(s == 0), stop=(s == BLOCKS - 1)
                        )
                for m, bank in banks.items():
                    nc.scalar.activation(h[0][m][:], bank[:], TANH, bias=bias1[:, m : m + 1], scale=1.0 / TOKENS)

        def step_b(r):
            for m in range(BLOCKS):
                bank = psum.tile([P, TOKENS], F32, name="bank", tag="right")
                for s in range(BLOCKS):
                    nc.tensor.matmul(
                        bank[:], y[r][s][:, block(m)], mask[s][:], start=(s == 0), stop=(s == BLOCKS - 1)
                    )
                nc.scalar.activation(h[r][m][:], bank[:], TANH, bias=bias1[:, m : m + 1], scale=1.0 / TOKENS)

        def step_c(r):
            half, quarter = TOKENS // 2, TOKENS // 4
            for e in range(BLOCKS):
                first = 0
                for width in (half, quarter, quarter) if (r, e) == (TEXTS - 1, BLOCKS - 1) else (TOKENS,):
                    t = slice(first, first + width)
                    bank = psum.tile([P, width], F32, name="bank", tag="left")
                    for m in range(BLOCKS):
                        nc.tensor.matmul(
                            bank[:], weights2[m][:, block(e)], h[r][m][:, t], start=(m == 0), stop=(m == BLOCKS - 1)
                        )
                    nc.scalar.activation(result[r][e][:, t], bank[:], TANH, bias=bias2[:, e : e + 1])
                    nc.sync.dma_start(out[block(e), r * TOKENS + t.start : r * TOKENS + t.stop], result[r][e][:, t])
                    first += width

        for d in range(BLOCKS):
            for c in column_parts(FEATURES, FIRST_PARTS if d == 0 else 1):
                nc.vector.tensor_tensor(weights1[d][:, c], slow1[d][:, c], fast1[d][:, c], ADD)
        for d in range(BLOCKS):
            for r, i in EARLY_PIECES:
                look_up(r, d, i, held.tile([P, PIECE], F32, name=f"picked{r}_{d}_{i}")[:])
        step_a(EARLY_PIECES)
        for s in range(BLOCKS):
            i, k = divmod(s, blocks_of_a_slot)
            nc.scalar.activation(mask[s][:], coherence[i][:, k * TOKENS : (k + 1) * TOKENS], SIGMOID)
        first_step_b()
        for m in range(BLOCKS):
            nc.vector.tensor_tensor(weights2[m][:], slow2[m][:], fast2[m][:], ADD)
        for n, (r, i) in enumerate(MIDDLE_PIECES):
            picked = reused.tile([P, BLOCKS * PIECE], F32, name=f"picked{r}_{i}", tag=f"coh{n % PIECES}")
            for d in range(BLOCKS):
                look_up(r, d, i, picked[:, d * PIECE : (d + 1) * PIECE])
            step_a([(r, i)])
        step_b(1)
        for r, i in LAST_PIECES:
            for d in range(BLOCKS):
                look_up(r, d, i, reused.tile([P, PIECE], F32, name=f"picked{r}_{d}_{i}", tag=f"y{d}")[:])
            step_a([(r, i)])
        step_c(0)
        for r in range(2, TEXTS):
            step_b(r)
            step_c(r - 1)
        step_c(TEXTS - 1)
